import numpy as np
import ml_dtypes


def mxq(x, axis, fmt="e4m3"):
    dtype, down = {"e4m3": (ml_dtypes.float8_e4m3fn, 7), "e5m2": (ml_dtypes.float8_e5m2, 14)}[fmt]
    v = np.moveaxis(np.asarray(x, np.float32).astype(ml_dtypes.bfloat16).astype(np.float64), axis, -1)
    blocks = v.reshape(v.shape[:-1] + (-1, 32))
    amax = np.abs(blocks).max(-1, keepdims=True)
    byte = np.maximum(np.where(amax > 0, np.frexp(amax)[1] - 1 + 127, 0) - down, 1)
    scale = np.exp2(byte - 127.0)
    codes = (blocks / scale).astype(np.float32).astype(dtype).astype(np.float64)
    return np.moveaxis((codes * scale).reshape(v.shape), -1, axis)


WIDE = False


def mx_kscale(k):
    if not WIDE:
        return np.ones(k)
    levels = np.array([10, -10, 5, -5, 0])
    a = np.random.permutation(np.resize(levels, k // 512 * 4)).reshape(k // 512, 4)
    idx = np.arange(k)
    return np.exp2(a[idx // 512, idx % 128 // 32])


BF16 = ml_dtypes.bfloat16


def bf(x):
    return np.asarray(x, np.float32).astype(BF16)


def f64(x):
    return np.asarray(x).astype(np.float64)


N, K, D_IN, HC, H = 256, 8, 1024, 1024, 1024


def sigmoid(v):
    return 1.0 / (1.0 + np.exp(-v))


def setup_inputs():
    s, t = mx_kscale(D_IN), mx_kscale(HC)
    return {
        "x": bf(np.random.standard_normal((N, D_IN)) * s),
        "child_h": bf(np.random.standard_normal((N, K, HC)) * t),
        "child_c": bf(np.random.standard_normal((N, K, H)) * 0.5),
        "Wf": bf(np.random.standard_normal((D_IN, H)) * 0.7 / np.sqrt(D_IN) / s[:, None]),
        "bWf": bf(np.random.standard_normal(H) * 0.3),
        "Uf": bf(np.random.standard_normal((HC, H)) * 0.7 / np.sqrt(HC) / t[:, None]),
        "bUf": bf(np.random.standard_normal(H) * 0.3),
    }


def reference(x, child_h, child_c, Wf, bWf, Uf, bUf):
    xf = (mxq(f64(x), 1, "e4m3") @ mxq(f64(Wf), 0, "e4m3")) + f64(bWf)
    hf = mxq(f64(child_h), 2, "e4m3") @ mxq(f64(Uf), 0, "e4m3")
    f = sigmoid(xf[:, None, :] + hf + f64(bUf))
    return (f * f64(child_c)).sum(axis=1)

@@ -1,0 +1,218 @@
+from contextlib import ExitStack
+
+import concourse.mybir as mybir
+from concourse.masks import make_identity
+
+F32 = mybir.dt.float32
+BF16 = mybir.dt.bfloat16
+U32 = mybir.dt.uint32
+U8 = mybir.dt.uint8
+FP8X4 = mybir.dt.float8_e4m3fn_x4
+ADD = mybir.AluOpType.add
+MULT = mybir.AluOpType.mult
+SIGMOID = mybir.ActivationFunctionType.Sigmoid
+
+P = 128
+NODES = 256
+CHILDREN = 8
+D = 1024
+H = 1024
+PACK = 4
+K_PASS = P * PACK
+PASSES = D // K_PASS
+PAIR_ROWS = 2 * P
+N_TILE = 512
+H_HALVES = H // N_TILE
+NODE_BLOCKS = NODES // P
+BLOCKS = N_TILE // P
+
+FLOPS = 2 * (NODES + NODES * CHILDREN) * D * H
+
+
+def load_weight_half(nc, pool, w, cols):
+    raw = pool.tile([P, PASSES, PACK, N_TILE], BF16, name="w_raw")
+    for g in range(PASSES):
+        for u in range(2):
+            first = K_PASS * g + PAIR_ROWS * u
+            nc.sync.dma_start(
+                out=raw[:, g, 2 * u : 2 * u + 2, :],
+                in_=w[first : first + PAIR_ROWS, cols].rearrange("(q e) c -> q e c", e=2),
+            )
+    return raw
+
+
+def quantise_weight_half(nc, stage, raw, codes, scales):
+    for g in range(PASSES):
+        grouped = stage.tile([P, N_TILE, PACK], BF16, name="w_grouped", align_bytes=64)
+        nc.scalar.copy(out=grouped[:], in_=raw[:, g].rearrange("p t c -> p c t"))
+        nc.vector.quantize_mx(
+            out=codes[:, g, :].bitcast(FP8X4),
+            scales=scales[:, g, :],
+            in_=grouped[:].rearrange("p c t -> p (c t)"),
+        )
+
+
+def transpose_and_quantise(nc, psum, stage, words, ident, codes, scales):
+    turned = psum.tile([P, PASSES, 2, P], F32, name="turned")
+    for g in range(PASSES):
+        for u in range(2):
+            first = (2 * g + u) * P
+            nc.tensor.transpose(turned[:, g, u, :], words[:, first : first + P], ident[:])
+    grouped = stage.tile([P, PASSES * P * PACK], BF16, name="a_grouped", align_bytes=64)
+    nc.scalar.copy(
+        out=grouped[:].bitcast(F32).rearrange("p (g r u) -> p g r u", g=PASSES, u=2),
+        in_=turned[:].rearrange("p g u r -> p g r u"),
+    )
+    nc.vector.quantize_mx(
+        out=codes.rearrange("p g r -> p (g r)").bitcast(FP8X4),
+        scales=scales.rearrange("p g r -> p (g r)"),
+        in_=grouped[:],
+    )
+
+
+def mx_product(nc, acc, a_codes, a_scales, w_codes, w_scales):
+    for g in range(PASSES):
+        nc.tensor.matmul_mx(
+            out=acc,
+            lhsT=a_codes[:, g, :].bitcast(FP8X4),
+            lhsT_scale=a_scales[:, g, :],
+            rhs=w_codes[:, g, :].bitcast(FP8X4),
+            rhs_scale=w_scales[:, g, :],
+            start=(g == 0),
+            stop=(g == PASSES - 1),
+        )
+
+
+def tile_childsumtreelstmcell_pa_kernel(tc, x, child_h, child_c, Wf, bWf, Uf, bUf, out):
+    nc = tc.nc
+    with ExitStack() as stack:
+        const = stack.enter_context(tc.tile_pool(name="const", bufs=1))
+        inputs = stack.enter_context(tc.tile_pool(name="inputs", bufs=1))
+        raws = stack.enter_context(tc.tile_pool(name="raws", bufs=2 * H_HALVES))
+        cells = stack.enter_context(tc.tile_pool(name="cells", bufs=H_HALVES * NODE_BLOCKS))
+        keep = stack.enter_context(tc.tile_pool(name="keep", bufs=1))
+        stage = stack.enter_context(tc.tile_pool(name="stage", bufs=2))
+        work = stack.enter_context(tc.tile_pool(name="work", bufs=3))
+        wide = stack.enter_context(tc.tile_pool(name="wide", bufs=2))
+        psum_turn = stack.enter_context(tc.psum_pool(name="psum_turn", bufs=2))
+        psum_acc = stack.enter_context(tc.psum_pool(name="psum_acc", bufs=4))
+        psum_sum = stack.enter_context(tc.psum_pool(name="psum_sum", bufs=1))
+
+        halves = [slice(N_TILE * hh, N_TILE * (hh + 1)) for hh in range(H_HALVES)]
+        node_rows = [slice(P * nb, P * (nb + 1)) for nb in range(NODE_BLOCKS)]
+
+        ident = const.tile([P, P], F32, name="ident")
+        make_identity(nc, ident[:])
+        ones = const.tile([P, P], BF16, name="ones")
+        nc.vector.memset(ones[:], 1.0)
+        bias_rows = const.tile([P, H], BF16, name="bias_rows")
+        nc.vector.memset(bias_rows[:], 0.0)
+
+        x_sb = inputs.tile([P, NODE_BLOCKS * D], BF16, name="x_sb")
+        nc.sync.dma_start(
+            out=x_sb[:].rearrange("p (b d) -> p b d", b=NODE_BLOCKS),
+            in_=x.rearrange("(b p) d -> p b d", p=P),
+        )
+        nc.sync.dma_start(out=bias_rows[0:1, :], in_=bWf.unsqueeze(0))
+        nc.sync.dma_start(out=bias_rows[1:2, :], in_=bUf.unsqueeze(0))
+        h_sb = [inputs.tile([P, CHILDREN * D], BF16, name="h_sb%d" % nb) for nb in range(NODE_BLOCKS)]
+        wf_raw = {}
+        uf_raw = {}
+        c_sb = {}
+
+        def load_children(nb):
+            for part in range(2):
+                kids = slice(CHILDREN // 2 * part, CHILDREN // 2 * (part + 1))
+                nc.sync.dma_start(
+                    out=h_sb[nb][:].rearrange("p (k d) -> p k d", k=CHILDREN)[:, kids, :],
+                    in_=child_h[node_rows[nb], kids, :],
+                )
+
+        def load_cells(hh, nb):
+            c_sb[hh, nb] = cells.tile([P, CHILDREN, N_TILE], BF16, name="c_sb")
+            nc.sync.dma_start(out=c_sb[hh, nb][:], in_=child_c[node_rows[nb], :, halves[hh]])
+
+        wf_raw[0] = load_weight_half(nc, raws, Wf, halves[0])
+        uf_raw[0] = load_weight_half(nc, raws, Uf, halves[0])
+        load_children(0)
+        load_cells(0, 0)
+        load_children(1)
+        load_cells(0, 1)
+        wf_raw[1] = load_weight_half(nc, raws, Wf, halves[1])
+        uf_raw[1] = load_weight_half(nc, raws, Uf, halves[1])
+        load_cells(1, 0)
+        load_cells(1, 1)
+
+        wf_codes = keep.tile([P, H_HALVES, PASSES, N_TILE], U32, name="wf_codes", align_bytes=64)
+        wf_scales = keep.tile([P, H_HALVES, PASSES, N_TILE], U8, name="wf_scales", align_bytes=64)
+        uf_codes = keep.tile([P, H_HALVES, PASSES, N_TILE], U32, name="uf_codes", align_bytes=64)
+        uf_scales = keep.tile([P, H_HALVES, PASSES, N_TILE], U8, name="uf_scales", align_bytes=64)
+        x_codes = keep.tile([P, NODE_BLOCKS, PASSES, P], U32, name="x_codes", align_bytes=64)
+        x_scales = keep.tile([P, NODE_BLOCKS, PASSES, P], U8, name="x_scales", align_bytes=64)
+        h_codes = keep.tile([P, NODE_BLOCKS, CHILDREN, PASSES, P], U32, name="h_codes", align_bytes=64)
+        h_scales = keep.tile([P, NODE_BLOCKS, CHILDREN, PASSES, P], U8, name="h_scales", align_bytes=64)
+
+        bias_sb = keep.tile([P, H], F32, name="bias_sb")
+        for hh in range(H_HALVES):
+            bias_ps = psum_acc.tile([P, N_TILE], F32, name="acc")
+            nc.tensor.matmul(out=bias_ps[:], lhsT=ones[:], rhs=bias_rows[:, halves[hh]], start=True, stop=True)
+            nc.scalar.copy(out=bias_sb[:, halves[hh]], in_=bias_ps[:])
+
+        words_per_row = D // 2
+        x_words = x_sb[:].bitcast(F32)
+        for nb in range(NODE_BLOCKS):
+            transpose_and_quantise(
+                nc, psum_turn, stage, x_words[:, words_per_row * nb : words_per_row * (nb + 1)], ident,
+                x_codes[:, nb], x_scales[:, nb],
+            )
+
+        def prepare_children(nb):
+            h_words = h_sb[nb][:].bitcast(F32)
+            for k in range(CHILDREN):
+                transpose_and_quantise(
+                    nc, psum_turn, stage, h_words[:, words_per_row * k : words_per_row * (k + 1)], ident,
+                    h_codes[:, nb, k], h_scales[:, nb, k],
+                )
+
+        xfb = keep.tile([P, NODE_BLOCKS, H], F32, name="xfb")
+
+        for hh in range(H_HALVES):
+            quantise_weight_half(nc, stage, wf_raw[hh], wf_codes[:, hh], wf_scales[:, hh])
+            quantise_weight_half(nc, stage, uf_raw[hh], uf_codes[:, hh], uf_scales[:, hh])
+            for nb in range(NODE_BLOCKS):
+                if hh == 0:
+                    prepare_children(nb)
+
+                xf_ps = psum_acc.tile([P, N_TILE], F32, name="acc")
+                mx_product(nc, xf_ps[:], x_codes[:, nb], x_scales[:, nb], wf_codes[:, hh], wf_scales[:, hh])
+                nc.vector.tensor_tensor(out=xfb[:, nb, halves[hh]], in0=xf_ps[:], in1=bias_sb[:, halves[hh]], op=ADD)
+
+                weighted = wide.tile([P, CHILDREN, N_TILE], F32, name="weighted")
+                for k in range(CHILDREN):
+                    hf_ps = psum_acc.tile([P, N_TILE], F32, name="acc")
+                    mx_product(nc, hf_ps[:], h_codes[:, nb, k], h_scales[:, nb, k], uf_codes[:, hh], uf_scales[:, hh])
+                    z = work.tile([P, N_TILE], F32, name="z")
+                    nc.vector.tensor_tensor(out=z[:], in0=hf_ps[:], in1=xfb[:, nb, halves[hh]], op=ADD)
+                    gate = work.tile([P, N_TILE], F32, name="gate")
+                    nc.scalar.activation(out=gate[:], in_=z[:], func=SIGMOID)
+                    nc.vector.tensor_tensor(out=weighted[:, k, :], in0=gate[:], in1=c_sb[hh, nb][:, k, :], op=MULT)
+
+                summed_t = psum_sum.tile([P, BLOCKS, P], F32, name="summed_t")
+                for j in range(BLOCKS):
+                    for k in range(CHILDREN):
+                        nc.tensor.matmul(
+                            out=summed_t[:, j, :],
+                            lhsT=weighted[:, k, P * j : P * (j + 1)],
+                            rhs=ident[:],
+                            is_transpose=True,
+                            start=(k == 0),
+                            stop=(k == CHILDREN - 1),
+                        )
+                summed_t_sb = work.tile([P, BLOCKS, P], F32, name="summed_t_sb")
+                nc.scalar.copy(out=summed_t_sb[:], in_=summed_t[:])
+                result_ps = psum_sum.tile([P, N_TILE], F32, name="result_ps")
+                for j in range(BLOCKS):
+                    nc.tensor.transpose(result_ps[:, P * j : P * (j + 1)], summed_t_sb[:, j, :], ident[:])
+                result = work.tile([P, N_TILE], F32, name="result")
+                nc.scalar.copy(out=result[:], in_=result_ps[:])
+                nc.sync.dma_start(out=out[node_rows[nb], halves[hh]], in_=result[:])

@@ -27,6 +27,8 @@ NODE_BLOCKS = NODES // P
 BLOCKS = N_TILE // P
 
 FLOPS = 2 * (NODES + NODES * CHILDREN) * D * H
+VECTOR_COLS = 256
+AHEAD = 4
 
 
 def load_weight_half(nc, pool, w, cols):
@@ -41,15 +43,21 @@ def load_weight_half(nc, pool, w, cols):
     return raw
 
 
-def quantise_weight_half(nc, stage, raw, codes, scales):
-    for g in range(PASSES):
-        grouped = stage.tile([P, N_TILE, PACK], BF16, name="w_grouped", align_bytes=64)
-        nc.scalar.copy(out=grouped[:], in_=raw[:, g].rearrange("p t c -> p c t"))
-        nc.vector.quantize_mx(
-            out=codes[:, g, :].bitcast(FP8X4),
-            scales=scales[:, g, :],
-            in_=grouped[:].rearrange("p c t -> p (c t)"),
-        )
+def quantise_weight_pass(nc, stage, raw_pass, codes, scales):
+    grouped = stage.tile([P, N_TILE, PACK], BF16, name="w_grouped", align_bytes=64)
+    nc.vector.tensor_copy(
+        out=grouped[:, :VECTOR_COLS, :].rearrange("p (c i) t -> p c t i", i=4),
+        in_=raw_pass[:, :, :VECTOR_COLS].rearrange("p t (c i) -> p c t i", i=4),
+    )
+    nc.scalar.copy(
+        out=grouped[:, VECTOR_COLS:, :].rearrange("p (c i) t -> p c t i", i=4),
+        in_=raw_pass[:, :, VECTOR_COLS:].rearrange("p t (c i) -> p c t i", i=4),
+    )
+    nc.vector.quantize_mx(
+        out=codes.bitcast(FP8X4),
+        scales=scales,
+        in_=grouped[:].rearrange("p c t -> p (c t)"),
+    )
 
 
 def transpose_and_quantise(nc, psum, stage, words, ident, codes, scales):
@@ -91,9 +99,8 @@ def tile_childsumtreelstmcell_pa_kernel(tc, x, child_h, child_c, Wf, bWf, Uf, bU
         raws = stack.enter_context(tc.tile_pool(name="raws", bufs=2 * H_HALVES))
         cells = stack.enter_context(tc.tile_pool(name="cells", bufs=H_HALVES * NODE_BLOCKS))
         keep = stack.enter_context(tc.tile_pool(name="keep", bufs=1))
-        stage = stack.enter_context(tc.tile_pool(name="stage", bufs=2))
+        stage = stack.enter_context(tc.tile_pool(name="stage", bufs=3))
         work = stack.enter_context(tc.tile_pool(name="work", bufs=3))
-        wide = stack.enter_context(tc.tile_pool(name="wide", bufs=2))
         psum_turn = stack.enter_context(tc.psum_pool(name="psum_turn", bufs=2))
         psum_acc = stack.enter_context(tc.psum_pool(name="psum_acc", bufs=4))
         psum_sum = stack.enter_context(tc.psum_pool(name="psum_sum", bufs=1))
@@ -109,48 +116,58 @@ def tile_childsumtreelstmcell_pa_kernel(tc, x, child_h, child_c, Wf, bWf, Uf, bU
         nc.vector.memset(bias_rows[:], 0.0)
 
         x_sb = inputs.tile([P, NODE_BLOCKS * D], BF16, name="x_sb")
+        h_sb = [inputs.tile([P, CHILDREN * D], BF16, name="h_sb%d" % nb) for nb in range(NODE_BLOCKS)]
+        w_raw = {}
+        c_sb = {}
+
+        def load_children(nb, part):
+            kids = slice(CHILDREN // 2 * part, CHILDREN // 2 * (part + 1))
+            nc.sync.dma_start(
+                out=h_sb[nb][:].rearrange("p (k d) -> p k d", k=CHILDREN)[:, kids, :],
+                in_=child_h[node_rows[nb], kids, :],
+            )
+
+        def load_cells(hh, nb):
+            c_sb[hh, nb] = cells.tile([P, CHILDREN, N_TILE], BF16, name="c_sb")
+            nc.sync.dma_start(out=c_sb[hh, nb][:], in_=child_c[node_rows[nb], :, halves[hh]])
+
         nc.sync.dma_start(
             out=x_sb[:].rearrange("p (b d) -> p b d", b=NODE_BLOCKS),
             in_=x.rearrange("(b p) d -> p b d", p=P),
         )
         nc.sync.dma_start(out=bias_rows[0:1, :], in_=bWf.unsqueeze(0))
         nc.sync.dma_start(out=bias_rows[1:2, :], in_=bUf.unsqueeze(0))
-        h_sb = [inputs.tile([P, CHILDREN * D], BF16, name="h_sb%d" % nb) for nb in range(NODE_BLOCKS)]
-        wf_raw = {}
-        uf_raw = {}
-        c_sb = {}
-
-        def load_children(nb):
-            for part in range(2):
-                kids = slice(CHILDREN // 2 * part, CHILDREN // 2 * (part + 1))
-                nc.sync.dma_start(
-                    out=h_sb[nb][:].rearrange("p (k d) -> p k d", k=CHILDREN)[:, kids, :],
-                    in_=child_h[node_rows[nb], kids, :],
-                )
-
-        def load_cells(hh, nb):
-            c_sb[hh, nb] = cells.tile([P, CHILDREN, N_TILE], BF16, name="c_sb")
-            nc.sync.dma_start(out=c_sb[hh, nb][:], in_=child_c[node_rows[nb], :, halves[hh]])
-
-        wf_raw[0] = load_weight_half(nc, raws, Wf, halves[0])
-        uf_raw[0] = load_weight_half(nc, raws, Uf, halves[0])
-        load_children(0)
+        w_raw["wf", 0] = load_weight_half(nc, raws, Wf, halves[0])
+        w_raw["uf", 0] = load_weight_half(nc, raws, Uf, halves[0])
+        load_children(0, 0)
         load_cells(0, 0)
-        load_children(1)
+        load_children(0, 1)
+        w_raw["wf", 1] = load_weight_half(nc, raws, Wf, halves[1])
+        load_children(1, 0)
         load_cells(0, 1)
-        wf_raw[1] = load_weight_half(nc, raws, Wf, halves[1])
-        uf_raw[1] = load_weight_half(nc, raws, Uf, halves[1])
+        w_raw["uf", 1] = load_weight_half(nc, raws, Uf, halves[1])
+        load_children(1, 1)
         load_cells(1, 0)
         load_cells(1, 1)
 
-        wf_codes = keep.tile([P, H_HALVES, PASSES, N_TILE], U32, name="wf_codes", align_bytes=64)
-        wf_scales = keep.tile([P, H_HALVES, PASSES, N_TILE], U8, name="wf_scales", align_bytes=64)
-        uf_codes = keep.tile([P, H_HALVES, PASSES, N_TILE], U32, name="uf_codes", align_bytes=64)
-        uf_scales = keep.tile([P, H_HALVES, PASSES, N_TILE], U8, name="uf_scales", align_bytes=64)
+        w_codes = {}
+        w_scales = {}
+        for name in ("wf", "uf"):
+            w_codes[name] = keep.tile([P, H_HALVES, PASSES, N_TILE], U32, name=name + "_codes", align_bytes=64)
+            w_scales[name] = keep.tile([P, H_HALVES, PASSES, N_TILE], U8, name=name + "_scales", align_bytes=64)
         x_codes = keep.tile([P, NODE_BLOCKS, PASSES, P], U32, name="x_codes", align_bytes=64)
         x_scales = keep.tile([P, NODE_BLOCKS, PASSES, P], U8, name="x_scales", align_bytes=64)
         h_codes = keep.tile([P, NODE_BLOCKS, CHILDREN, PASSES, P], U32, name="h_codes", align_bytes=64)
         h_scales = keep.tile([P, NODE_BLOCKS, CHILDREN, PASSES, P], U8, name="h_scales", align_bytes=64)
+
+        def prepare_weight_pass(name, hh, g):
+            quantise_weight_pass(nc, stage, w_raw[name, hh][:, g], w_codes[name][:, hh, g, :], w_scales[name][:, hh, g, :])
+
+        words_per_row = D // 2
+
+        def prepare_child(nb, k):
+            words = h_sb[nb][:].bitcast(F32)[:, words_per_row * k : words_per_row * (k + 1)]
+            transpose_and_quantise(nc, psum_turn, stage, words, ident, h_codes[:, nb, k], h_scales[:, nb, k])
 
         bias_sb = keep.tile([P, H], F32, name="bias_sb")
         for hh in range(H_HALVES):
@@ -158,56 +175,56 @@ def tile_childsumtreelstmcell_pa_kernel(tc, x, child_h, child_c, Wf, bWf, Uf, bU
             nc.tensor.matmul(out=bias_ps[:], lhsT=ones[:], rhs=bias_rows[:, halves[hh]], start=True, stop=True)
             nc.scalar.copy(out=bias_sb[:, halves[hh]], in_=bias_ps[:])
 
-        words_per_row = D // 2
-        x_words = x_sb[:].bitcast(F32)
         for nb in range(NODE_BLOCKS):
-            transpose_and_quantise(
-                nc, psum_turn, stage, x_words[:, words_per_row * nb : words_per_row * (nb + 1)], ident,
-                x_codes[:, nb], x_scales[:, nb],
-            )
-
-        def prepare_children(nb):
-            h_words = h_sb[nb][:].bitcast(F32)
-            for k in range(CHILDREN):
-                transpose_and_quantise(
-                    nc, psum_turn, stage, h_words[:, words_per_row * k : words_per_row * (k + 1)], ident,
-                    h_codes[:, nb, k], h_scales[:, nb, k],
-                )
+            words = x_sb[:].bitcast(F32)[:, words_per_row * nb : words_per_row * (nb + 1)]
+            transpose_and_quantise(nc, psum_turn, stage, words, ident, x_codes[:, nb], x_scales[:, nb])
+        for name in ("wf", "uf"):
+            for g in range(PASSES):
+                prepare_weight_pass(name, 0, g)
+        for k in range(AHEAD):
+            prepare_child(0, k)
 
         xfb = keep.tile([P, NODE_BLOCKS, H], F32, name="xfb")
+        pairs_per_block = CHILDREN // 2
+        summed_t = None
 
-        for hh in range(H_HALVES):
-            quantise_weight_half(nc, stage, wf_raw[hh], wf_codes[:, hh], wf_scales[:, hh])
-            quantise_weight_half(nc, stage, uf_raw[hh], uf_codes[:, hh], uf_scales[:, hh])
-            for nb in range(NODE_BLOCKS):
-                if hh == 0:
-                    prepare_children(nb)
+        for pair in range(H_HALVES * NODE_BLOCKS * pairs_per_block):
+            hh = pair // (NODE_BLOCKS * pairs_per_block)
+            nb = pair // pairs_per_block % NODE_BLOCKS
+            first_child = 2 * (pair % pairs_per_block)
 
+            if first_child == 0:
                 xf_ps = psum_acc.tile([P, N_TILE], F32, name="acc")
-                mx_product(nc, xf_ps[:], x_codes[:, nb], x_scales[:, nb], wf_codes[:, hh], wf_scales[:, hh])
+                mx_product(nc, xf_ps[:], x_codes[:, nb], x_scales[:, nb], w_codes["wf"][:, hh], w_scales["wf"][:, hh])
                 nc.vector.tensor_tensor(out=xfb[:, nb, halves[hh]], in0=xf_ps[:], in1=bias_sb[:, halves[hh]], op=ADD)
-
-                weighted = wide.tile([P, CHILDREN, N_TILE], F32, name="weighted")
-                for k in range(CHILDREN):
-                    hf_ps = psum_acc.tile([P, N_TILE], F32, name="acc")
-                    mx_product(nc, hf_ps[:], h_codes[:, nb, k], h_scales[:, nb, k], uf_codes[:, hh], uf_scales[:, hh])
-                    z = work.tile([P, N_TILE], F32, name="z")
-                    nc.vector.tensor_tensor(out=z[:], in0=hf_ps[:], in1=xfb[:, nb, halves[hh]], op=ADD)
-                    gate = work.tile([P, N_TILE], F32, name="gate")
-                    nc.scalar.activation(out=gate[:], in_=z[:], func=SIGMOID)
-                    nc.vector.tensor_tensor(out=weighted[:, k, :], in0=gate[:], in1=c_sb[hh, nb][:, k, :], op=MULT)
-
                 summed_t = psum_sum.tile([P, BLOCKS, P], F32, name="summed_t")
+
+            z = work.tile([P, 2, N_TILE], F32, name="z")
+            for i in range(2):
+                k = first_child + i
+                hf_ps = psum_acc.tile([P, N_TILE], F32, name="acc")
+                mx_product(nc, hf_ps[:], h_codes[:, nb, k], h_scales[:, nb, k], w_codes["uf"][:, hh], w_scales["uf"][:, hh])
+                nc.vector.tensor_tensor(out=z[:, i, :], in0=hf_ps[:], in1=xfb[:, nb, halves[hh]], op=ADD)
+            gate = work.tile([P, 2, N_TILE], F32, name="gate")
+            nc.scalar.activation(out=gate[:], in_=z[:], func=SIGMOID)
+            weighted = work.tile([P, 2, N_TILE], F32, name="weighted")
+            nc.vector.tensor_tensor(
+                out=weighted[:], in0=gate[:], in1=c_sb[hh, nb][:, first_child : first_child + 2, :], op=MULT
+            )
+
+            for i in range(2):
+                k = first_child + i
                 for j in range(BLOCKS):
-                    for k in range(CHILDREN):
-                        nc.tensor.matmul(
-                            out=summed_t[:, j, :],
-                            lhsT=weighted[:, k, P * j : P * (j + 1)],
-                            rhs=ident[:],
-                            is_transpose=True,
-                            start=(k == 0),
-                            stop=(k == CHILDREN - 1),
-                        )
+                    nc.tensor.matmul(
+                        out=summed_t[:, j, :],
+                        lhsT=weighted[:, i, P * j : P * (j + 1)],
+                        rhs=ident[:],
+                        is_transpose=True,
+                        start=(k == 0 and j == 0),
+                        stop=(k == CHILDREN - 1 and j == BLOCKS - 1),
+                    )
+
+            if first_child == CHILDREN - 2:
                 summed_t_sb = work.tile([P, BLOCKS, P], F32, name="summed_t_sb")
                 nc.scalar.copy(out=summed_t_sb[:], in_=summed_t[:])
                 result_ps = psum_sum.tile([P, N_TILE], F32, name="result_ps")
@@ -216,3 +233,10 @@ def tile_childsumtreelstmcell_pa_kernel(tc, x, child_h, child_c, Wf, bWf, Uf, bU
                 result = work.tile([P, N_TILE], F32, name="result")
                 nc.scalar.copy(out=result[:], in_=result_ps[:])
                 nc.sync.dma_start(out=out[node_rows[nb], halves[hh]], in_=result[:])
+
+            for i in range(2):
+                child = 2 * pair + i + AHEAD
+                if child < NODE_BLOCKS * CHILDREN:
+                    prepare_child(child // CHILDREN, child % CHILDREN)
+            if hh == 0 and pair % 2 == 1:
+                prepare_weight_pass(("wf", "uf")[pair // 4], 1, pair // 2 % PASSES)

@@ -28,67 +28,9 @@ BLOCKS = N_TILE // P
 
 FLOPS = 2 * (NODES + NODES * CHILDREN) * D * H
 VECTOR_COLS = 256
-AHEAD = 4
-
-
-def load_weight_half(nc, pool, w, cols):
-    raw = pool.tile([P, PASSES, PACK, N_TILE], BF16, name="w_raw")
-    for g in range(PASSES):
-        for u in range(2):
-            first = K_PASS * g + PAIR_ROWS * u
-            nc.sync.dma_start(
-                out=raw[:, g, 2 * u : 2 * u + 2, :],
-                in_=w[first : first + PAIR_ROWS, cols].rearrange("(q e) c -> q e c", e=2),
-            )
-    return raw
-
-
-def quantise_weight_pass(nc, stage, raw_pass, codes, scales):
-    grouped = stage.tile([P, N_TILE, PACK], BF16, name="w_grouped", align_bytes=64)
-    nc.vector.tensor_copy(
-        out=grouped[:, :VECTOR_COLS, :].rearrange("p (c i) t -> p c t i", i=4),
-        in_=raw_pass[:, :, :VECTOR_COLS].rearrange("p t (c i) -> p c t i", i=4),
-    )
-    nc.scalar.copy(
-        out=grouped[:, VECTOR_COLS:, :].rearrange("p (c i) t -> p c t i", i=4),
-        in_=raw_pass[:, :, VECTOR_COLS:].rearrange("p t (c i) -> p c t i", i=4),
-    )
-    nc.vector.quantize_mx(
-        out=codes.bitcast(FP8X4),
-        scales=scales,
-        in_=grouped[:].rearrange("p c t -> p (c t)"),
-    )
-
-
-def transpose_and_quantise(nc, psum, stage, words, ident, codes, scales):
-    turned = psum.tile([P, PASSES, 2, P], F32, name="turned")
-    for g in range(PASSES):
-        for u in range(2):
-            first = (2 * g + u) * P
-            nc.tensor.transpose(turned[:, g, u, :], words[:, first : first + P], ident[:])
-    grouped = stage.tile([P, PASSES * P * PACK], BF16, name="a_grouped", align_bytes=64)
-    nc.scalar.copy(
-        out=grouped[:].bitcast(F32).rearrange("p (g r u) -> p g r u", g=PASSES, u=2),
-        in_=turned[:].rearrange("p g u r -> p g r u"),
-    )
-    nc.vector.quantize_mx(
-        out=codes.rearrange("p g r -> p (g r)").bitcast(FP8X4),
-        scales=scales.rearrange("p g r -> p (g r)"),
-        in_=grouped[:],
-    )
-
-
-def mx_product(nc, acc, a_codes, a_scales, w_codes, w_scales):
-    for g in range(PASSES):
-        nc.tensor.matmul_mx(
-            out=acc,
-            lhsT=a_codes[:, g, :].bitcast(FP8X4),
-            lhsT_scale=a_scales[:, g, :],
-            rhs=w_codes[:, g, :].bitcast(FP8X4),
-            rhs_scale=w_scales[:, g, :],
-            start=(g == 0),
-            stop=(g == PASSES - 1),
-        )
+PAIRS_PER_UNIT = CHILDREN // 2
+PAIRS = H_HALVES * NODE_BLOCKS * PAIRS_PER_UNIT
+LATE_WEIGHTS = 2
 
 
 def tile_childsumtreelstmcell_pa_kernel(tc, x, child_h, child_c, Wf, bWf, Uf, bUf, out):
@@ -96,17 +38,17 @@ def tile_childsumtreelstmcell_pa_kernel(tc, x, child_h, child_c, Wf, bWf, Uf, bU
     with ExitStack() as stack:
         const = stack.enter_context(tc.tile_pool(name="const", bufs=1))
         inputs = stack.enter_context(tc.tile_pool(name="inputs", bufs=1))
-        raws = stack.enter_context(tc.tile_pool(name="raws", bufs=2 * H_HALVES))
-        cells = stack.enter_context(tc.tile_pool(name="cells", bufs=H_HALVES * NODE_BLOCKS))
         keep = stack.enter_context(tc.tile_pool(name="keep", bufs=1))
-        stage = stack.enter_context(tc.tile_pool(name="stage", bufs=3))
+        stage = stack.enter_context(tc.tile_pool(name="stage", bufs=2))
         work = stack.enter_context(tc.tile_pool(name="work", bufs=3))
         psum_turn = stack.enter_context(tc.psum_pool(name="psum_turn", bufs=2))
         psum_acc = stack.enter_context(tc.psum_pool(name="psum_acc", bufs=4))
-        psum_sum = stack.enter_context(tc.psum_pool(name="psum_sum", bufs=1))
+        psum_one = stack.enter_context(tc.psum_pool(name="psum_one", bufs=1))
+        stack.enter_context(tc.manual_schedule())
 
         halves = [slice(N_TILE * hh, N_TILE * (hh + 1)) for hh in range(H_HALVES)]
         node_rows = [slice(P * nb, P * (nb + 1)) for nb in range(NODE_BLOCKS)]
+        weights = {"wf": Wf, "uf": Uf}
 
         ident = const.tile([P, P], F32, name="ident")
         make_identity(nc, ident[:])
@@ -114,11 +56,27 @@ def tile_childsumtreelstmcell_pa_kernel(tc, x, child_h, child_c, Wf, bWf, Uf, bU
         nc.vector.memset(ones[:], 1.0)
         bias_rows = const.tile([P, H], BF16, name="bias_rows")
         nc.vector.memset(bias_rows[:], 0.0)
+        warm = const.tile([P, 1], F32, name="warm")
+        nc.scalar.activation(out=warm[:], in_=ones[:, 0:1], func=SIGMOID)
 
         x_sb = inputs.tile([P, NODE_BLOCKS * D], BF16, name="x_sb")
         h_sb = [inputs.tile([P, CHILDREN * D], BF16, name="h_sb%d" % nb) for nb in range(NODE_BLOCKS)]
-        w_raw = {}
         c_sb = {}
+        w_raw = {}
+        for hh in range(H_HALVES):
+            for nb in range(NODE_BLOCKS):
+                c_sb[hh, nb] = inputs.tile([P, CHILDREN, N_TILE], BF16, name="c_sb%d%d" % (hh, nb))
+            for name in weights:
+                w_raw[name, hh] = inputs.tile([P, PASSES, PACK, N_TILE], BF16, name="%s_raw%d" % (name, hh))
+
+        def load_weight_half(name, hh):
+            for g in range(PASSES):
+                for u in range(2):
+                    first = K_PASS * g + PAIR_ROWS * u
+                    nc.sync.dma_start(
+                        out=w_raw[name, hh][:, g, 2 * u : 2 * u + 2, :],
+                        in_=weights[name][first : first + PAIR_ROWS, halves[hh]].rearrange("(q e) c -> q e c", e=2),
+                    )
 
         def load_children(nb, part):
             kids = slice(CHILDREN // 2 * part, CHILDREN // 2 * (part + 1))
@@ -127,9 +85,9 @@ def tile_childsumtreelstmcell_pa_kernel(tc, x, child_h, child_c, Wf, bWf, Uf, bU
                 in_=child_h[node_rows[nb], kids, :],
             )
 
-        def load_cells(hh, nb):
-            c_sb[hh, nb] = cells.tile([P, CHILDREN, N_TILE], BF16, name="c_sb")
-            nc.sync.dma_start(out=c_sb[hh, nb][:], in_=child_c[node_rows[nb], :, halves[hh]])
+        def load_cells(hh, nb, part):
+            kids = slice(CHILDREN // 2 * part, CHILDREN // 2 * (part + 1))
+            nc.sync.dma_start(out=c_sb[hh, nb][:, kids, :], in_=child_c[node_rows[nb], kids, halves[hh]])
 
         nc.sync.dma_start(
             out=x_sb[:].rearrange("p (b d) -> p b d", b=NODE_BLOCKS),
@@ -137,106 +95,220 @@ def tile_childsumtreelstmcell_pa_kernel(tc, x, child_h, child_c, Wf, bWf, Uf, bU
         )
         nc.sync.dma_start(out=bias_rows[0:1, :], in_=bWf.unsqueeze(0))
         nc.sync.dma_start(out=bias_rows[1:2, :], in_=bUf.unsqueeze(0))
-        w_raw["wf", 0] = load_weight_half(nc, raws, Wf, halves[0])
-        w_raw["uf", 0] = load_weight_half(nc, raws, Uf, halves[0])
+        load_weight_half("wf", 0)
+        load_weight_half("uf", 0)
         load_children(0, 0)
-        load_cells(0, 0)
         load_children(0, 1)
-        w_raw["wf", 1] = load_weight_half(nc, raws, Wf, halves[1])
+        load_cells(0, 0, 0)
         load_children(1, 0)
-        load_cells(0, 1)
-        w_raw["uf", 1] = load_weight_half(nc, raws, Uf, halves[1])
+        load_cells(0, 0, 1)
+        load_weight_half("wf", 1)
         load_children(1, 1)
-        load_cells(1, 0)
-        load_cells(1, 1)
+        load_cells(0, 1, 0)
+        load_weight_half("uf", 1)
+        load_cells(0, 1, 1)
+        for nb in range(NODE_BLOCKS):
+            for part in range(2):
+                load_cells(1, nb, part)
 
         w_codes = {}
         w_scales = {}
-        for name in ("wf", "uf"):
+        for name in weights:
             w_codes[name] = keep.tile([P, H_HALVES, PASSES, N_TILE], U32, name=name + "_codes", align_bytes=64)
             w_scales[name] = keep.tile([P, H_HALVES, PASSES, N_TILE], U8, name=name + "_scales", align_bytes=64)
         x_codes = keep.tile([P, NODE_BLOCKS, PASSES, P], U32, name="x_codes", align_bytes=64)
         x_scales = keep.tile([P, NODE_BLOCKS, PASSES, P], U8, name="x_scales", align_bytes=64)
-        h_codes = keep.tile([P, NODE_BLOCKS, CHILDREN, PASSES, P], U32, name="h_codes", align_bytes=64)
-        h_scales = keep.tile([P, NODE_BLOCKS, CHILDREN, PASSES, P], U8, name="h_scales", align_bytes=64)
+        h_codes = keep.tile([P, NODE_BLOCKS * CHILDREN, PASSES, P], U32, name="h_codes", align_bytes=64)
+        h_scales = keep.tile([P, NODE_BLOCKS * CHILDREN, PASSES, P], U8, name="h_scales", align_bytes=64)
+        bias_sb = keep.tile([P, H], F32, name="bias_sb")
+        xfb = keep.tile([P, NODE_BLOCKS, H], F32, name="xfb")
 
-        def prepare_weight_pass(name, hh, g):
-            quantise_weight_pass(nc, stage, w_raw[name, hh][:, g], w_codes[name][:, hh, g, :], w_scales[name][:, hh, g, :])
-
+        turned = {}
+        a_grouped = {}
+        w_grouped = {}
+        acc = {}
+        z = {}
+        gate = {}
+        weighted = {}
+        summed_t = {}
+        summed_t_sb = {}
+        result_ps = {}
         words_per_row = D // 2
 
-        def prepare_child(nb, k):
-            words = h_sb[nb][:].bitcast(F32)[:, words_per_row * k : words_per_row * (k + 1)]
-            transpose_and_quantise(nc, psum_turn, stage, words, ident, h_codes[:, nb, k], h_scales[:, nb, k])
+        def turn(key, words):
+            for i in range(2):
+                turned[key, i] = psum_turn.tile([P, PASSES, 2, P], F32, name="turned")
+                for g in range(PASSES):
+                    for u in range(2):
+                        first = words_per_row * i + (2 * g + u) * P
+                        nc.tensor.transpose(turned[key, i][:, g, u, :], words[:, first : first + P], ident[:])
 
-        bias_sb = keep.tile([P, H], F32, name="bias_sb")
+        def regroup_turned(key):
+            a_grouped[key] = stage.tile([P, 2 * PASSES * P * PACK], BF16, name="a_grouped", align_bytes=64)
+            pairs_of_words = a_grouped[key][:].bitcast(F32).rearrange("p (i g r u) -> p i g r u", i=2, g=PASSES, u=2)
+            for i in range(2):
+                nc.scalar.copy(out=pairs_of_words[:, i], in_=turned[key, i][:].rearrange("p g u r -> p g r u"))
+
+        def quantise_turned(key, codes, scales):
+            nc.vector.quantize_mx(
+                out=codes.rearrange("p i g r -> p (i g r)").bitcast(FP8X4),
+                scales=scales.rearrange("p i g r -> p (i g r)"),
+                in_=a_grouped[key][:],
+            )
+
+        def weight_pass(piece):
+            return ("wf", "uf")[piece // PASSES % 2], piece // (2 * PASSES), piece % PASSES
+
+        def regroup_weights(piece):
+            name, hh, g = weight_pass(piece)
+            w_grouped[piece] = stage.tile([P, N_TILE, PACK], BF16, name="w_grouped", align_bytes=64)
+            nc.vector.tensor_copy(
+                out=w_grouped[piece][:, :VECTOR_COLS, :].rearrange("p (c i) t -> p c t i", i=4),
+                in_=w_raw[name, hh][:, g, :, :VECTOR_COLS].rearrange("p t (c i) -> p c t i", i=4),
+            )
+            nc.scalar.copy(
+                out=w_grouped[piece][:, VECTOR_COLS:, :].rearrange("p (c i) t -> p c t i", i=4),
+                in_=w_raw[name, hh][:, g, :, VECTOR_COLS:].rearrange("p t (c i) -> p c t i", i=4),
+            )
+
+        def quantise_weights(piece):
+            name, hh, g = weight_pass(piece)
+            nc.vector.quantize_mx(
+                out=w_codes[name][:, hh, g, :].bitcast(FP8X4),
+                scales=w_scales[name][:, hh, g, :],
+                in_=w_grouped[piece][:].rearrange("p c t -> p (c t)"),
+            )
+
+        def mx_product(bank, a_codes, a_scales, name, hh):
+            for g in range(PASSES):
+                nc.tensor.matmul_mx(
+                    out=bank,
+                    lhsT=a_codes[:, g, :].bitcast(FP8X4),
+                    lhsT_scale=a_scales[:, g, :],
+                    rhs=w_codes[name][:, hh, g, :].bitcast(FP8X4),
+                    rhs_scale=w_scales[name][:, hh, g, :],
+                    start=(g == 0),
+                    stop=(g == PASSES - 1),
+                )
+
+        def place(pair):
+            unit = pair // PAIRS_PER_UNIT
+            return unit, unit // NODE_BLOCKS, unit % NODE_BLOCKS, 2 * (pair % PAIRS_PER_UNIT)
+
+        def turn_children(pair):
+            if 0 <= pair < NODE_BLOCKS * PAIRS_PER_UNIT:
+                unit, hh, nb, first_child = place(pair)
+                turn(pair, h_sb[nb][:].bitcast(F32)[:, words_per_row * first_child : words_per_row * (first_child + 2)])
+
+        def regroup_children(pair):
+            if 0 <= pair < NODE_BLOCKS * PAIRS_PER_UNIT:
+                regroup_turned(pair)
+
+        def quantise_children(pair):
+            if 0 <= pair < NODE_BLOCKS * PAIRS_PER_UNIT:
+                quantise_turned(pair, h_codes[:, 2 * pair : 2 * pair + 2], h_scales[:, 2 * pair : 2 * pair + 2])
+
+        def multiply(pair):
+            if 0 <= pair < PAIRS:
+                unit, hh, nb, first_child = place(pair)
+                if first_child == 0:
+                    acc["x", unit] = psum_one.tile([P, N_TILE], F32, name="lone")
+                    mx_product(acc["x", unit][:], x_codes[:, nb], x_scales[:, nb], "wf", hh)
+                for i in range(2):
+                    child = CHILDREN * nb + first_child + i
+                    acc[pair, i] = psum_acc.tile([P, N_TILE], F32, name="acc")
+                    mx_product(acc[pair, i][:], h_codes[:, child], h_scales[:, child], "uf", hh)
+
+        def add_x(pair):
+            if 0 <= pair < PAIRS:
+                unit, hh, nb, first_child = place(pair)
+                if first_child == 0:
+                    nc.vector.tensor_tensor(
+                        out=xfb[:, nb, halves[hh]], in0=acc["x", unit][:], in1=bias_sb[:, halves[hh]], op=ADD
+                    )
+                z[pair] = work.tile([P, 2, N_TILE], F32, name="z")
+                for i in range(2):
+                    nc.vector.tensor_tensor(out=z[pair][:, i, :], in0=acc[pair, i][:], in1=xfb[:, nb, halves[hh]], op=ADD)
+
+        def squash(pair):
+            if 0 <= pair < PAIRS:
+                gate[pair] = work.tile([P, 2, N_TILE], F32, name="gate")
+                nc.scalar.activation(out=gate[pair][:], in_=z[pair][:], func=SIGMOID)
+
+        def weigh(pair):
+            if 0 <= pair < PAIRS:
+                unit, hh, nb, first_child = place(pair)
+                weighted[pair] = work.tile([P, 2, N_TILE], F32, name="weighted")
+                nc.vector.tensor_tensor(
+                    out=weighted[pair][:], in0=gate[pair][:], in1=c_sb[hh, nb][:, first_child : first_child + 2, :], op=MULT
+                )
+
+        def sum_children(pair):
+            if 0 <= pair < PAIRS:
+                unit, hh, nb, first_child = place(pair)
+                if first_child == 0:
+                    summed_t[unit] = psum_one.tile([P, BLOCKS, P], F32, name="summed_t")
+                for i in range(2):
+                    for j in range(BLOCKS):
+                        nc.tensor.matmul(
+                            out=summed_t[unit][:, j, :],
+                            lhsT=weighted[pair][:, i, P * j : P * (j + 1)],
+                            rhs=ident[:],
+                            is_transpose=True,
+                            start=(first_child + i == 0 and j == 0),
+                            stop=(first_child + i == CHILDREN - 1 and j == BLOCKS - 1),
+                        )
+
+        def is_last_of_unit(pair):
+            return 0 <= pair < PAIRS and pair % PAIRS_PER_UNIT == PAIRS_PER_UNIT - 1
+
+        def copy_sum(pair):
+            if is_last_of_unit(pair):
+                unit = pair // PAIRS_PER_UNIT
+                summed_t_sb[unit] = work.tile([P, BLOCKS, P], F32, name="summed_t_sb")
+                nc.scalar.copy(out=summed_t_sb[unit][:], in_=summed_t[unit][:])
+
+        def turn_sum_back(pair):
+            if is_last_of_unit(pair):
+                unit = pair // PAIRS_PER_UNIT
+                result_ps[unit] = psum_one.tile([P, N_TILE], F32, name="lone")
+                for j in range(BLOCKS):
+                    nc.tensor.transpose(result_ps[unit][:, P * j : P * (j + 1)], summed_t_sb[unit][:, j, :], ident[:])
+
+        def store(pair):
+            if is_last_of_unit(pair):
+                unit, hh, nb, first_child = place(pair)
+                result = work.tile([P, N_TILE], F32, name="result")
+                nc.scalar.copy(out=result[:], in_=result_ps[unit][:])
+                nc.sync.dma_start(out=out[node_rows[nb], halves[hh]], in_=result[:])
+
+        turn("x", x_sb[:].bitcast(F32))
+        regroup_turned("x")
+        quantise_turned("x", x_codes[:], x_scales[:])
         for hh in range(H_HALVES):
             bias_ps = psum_acc.tile([P, N_TILE], F32, name="acc")
             nc.tensor.matmul(out=bias_ps[:], lhsT=ones[:], rhs=bias_rows[:, halves[hh]], start=True, stop=True)
             nc.scalar.copy(out=bias_sb[:, halves[hh]], in_=bias_ps[:])
+        for piece in range(2 * PASSES + 1):
+            if piece < 2 * PASSES:
+                regroup_weights(piece)
+            if piece > 0:
+                quantise_weights(piece - 1)
 
-        for nb in range(NODE_BLOCKS):
-            words = x_sb[:].bitcast(F32)[:, words_per_row * nb : words_per_row * (nb + 1)]
-            transpose_and_quantise(nc, psum_turn, stage, words, ident, x_codes[:, nb], x_scales[:, nb])
-        for name in ("wf", "uf"):
-            for g in range(PASSES):
-                prepare_weight_pass(name, 0, g)
-        for k in range(AHEAD):
-            prepare_child(0, k)
-
-        xfb = keep.tile([P, NODE_BLOCKS, H], F32, name="xfb")
-        pairs_per_block = CHILDREN // 2
-        summed_t = None
-
-        for pair in range(H_HALVES * NODE_BLOCKS * pairs_per_block):
-            hh = pair // (NODE_BLOCKS * pairs_per_block)
-            nb = pair // pairs_per_block % NODE_BLOCKS
-            first_child = 2 * (pair % pairs_per_block)
-
-            if first_child == 0:
-                xf_ps = psum_acc.tile([P, N_TILE], F32, name="acc")
-                mx_product(nc, xf_ps[:], x_codes[:, nb], x_scales[:, nb], w_codes["wf"][:, hh], w_scales["wf"][:, hh])
-                nc.vector.tensor_tensor(out=xfb[:, nb, halves[hh]], in0=xf_ps[:], in1=bias_sb[:, halves[hh]], op=ADD)
-                summed_t = psum_sum.tile([P, BLOCKS, P], F32, name="summed_t")
-
-            z = work.tile([P, 2, N_TILE], F32, name="z")
-            for i in range(2):
-                k = first_child + i
-                hf_ps = psum_acc.tile([P, N_TILE], F32, name="acc")
-                mx_product(nc, hf_ps[:], h_codes[:, nb, k], h_scales[:, nb, k], w_codes["uf"][:, hh], w_scales["uf"][:, hh])
-                nc.vector.tensor_tensor(out=z[:, i, :], in0=hf_ps[:], in1=xfb[:, nb, halves[hh]], op=ADD)
-            gate = work.tile([P, 2, N_TILE], F32, name="gate")
-            nc.scalar.activation(out=gate[:], in_=z[:], func=SIGMOID)
-            weighted = work.tile([P, 2, N_TILE], F32, name="weighted")
-            nc.vector.tensor_tensor(
-                out=weighted[:], in0=gate[:], in1=c_sb[hh, nb][:, first_child : first_child + 2, :], op=MULT
-            )
-
-            for i in range(2):
-                k = first_child + i
-                for j in range(BLOCKS):
-                    nc.tensor.matmul(
-                        out=summed_t[:, j, :],
-                        lhsT=weighted[:, i, P * j : P * (j + 1)],
-                        rhs=ident[:],
-                        is_transpose=True,
-                        start=(k == 0 and j == 0),
-                        stop=(k == CHILDREN - 1 and j == BLOCKS - 1),
-                    )
-
-            if first_child == CHILDREN - 2:
-                summed_t_sb = work.tile([P, BLOCKS, P], F32, name="summed_t_sb")
-                nc.scalar.copy(out=summed_t_sb[:], in_=summed_t[:])
-                result_ps = psum_sum.tile([P, N_TILE], F32, name="result_ps")
-                for j in range(BLOCKS):
-                    nc.tensor.transpose(result_ps[:, P * j : P * (j + 1)], summed_t_sb[:, j, :], ident[:])
-                result = work.tile([P, N_TILE], F32, name="result")
-                nc.scalar.copy(out=result[:], in_=result_ps[:])
-                nc.sync.dma_start(out=out[node_rows[nb], halves[hh]], in_=result[:])
-
-            for i in range(2):
-                child = 2 * pair + i + AHEAD
-                if child < NODE_BLOCKS * CHILDREN:
-                    prepare_child(child // CHILDREN, child % CHILDREN)
-            if hh == 0 and pair % 2 == 1:
-                prepare_weight_pass(("wf", "uf")[pair // 4], 1, pair // 2 % PASSES)
+        for now in range(-4, PAIRS + 3):
+            sum_children(now - 1)
+            turn_sum_back(now - 2)
+            multiply(now + 2)
+            regroup_children(now + 3)
+            turn_children(now + 4)
+            add_x(now + 1)
+            late_piece = now + LATE_WEIGHTS
+            if 2 * PASSES <= late_piece < 4 * PASSES:
+                regroup_weights(late_piece)
+            squash(now + 1)
+            weigh(now)
+            quantise_children(now + 3)
+            if 2 * PASSES <= late_piece < 4 * PASSES:
+                quantise_weights(late_piece)
+            copy_sum(now - 1)
+            store(now - 2)

@@ -28,9 +28,67 @@ BLOCKS = N_TILE // P
 
 FLOPS = 2 * (NODES + NODES * CHILDREN) * D * H
 VECTOR_COLS = 256
-PAIRS_PER_UNIT = CHILDREN // 2
-PAIRS = H_HALVES * NODE_BLOCKS * PAIRS_PER_UNIT
-LATE_WEIGHTS = 2
+AHEAD = 6
+
+
+def load_weight_half(nc, pool, w, cols):
+    raw = pool.tile([P, PASSES, PACK, N_TILE], BF16, name="w_raw")
+    for g in range(PASSES):
+        for u in range(2):
+            first = K_PASS * g + PAIR_ROWS * u
+            nc.sync.dma_start(
+                out=raw[:, g, 2 * u : 2 * u + 2, :],
+                in_=w[first : first + PAIR_ROWS, cols].rearrange("(q e) c -> q e c", e=2),
+            )
+    return raw
+
+
+def quantise_weight_pass(nc, stage, raw_pass, codes, scales):
+    grouped = stage.tile([P, N_TILE, PACK], BF16, name="w_grouped", align_bytes=64)
+    nc.vector.tensor_copy(
+        out=grouped[:, :VECTOR_COLS, :].rearrange("p (c i) t -> p c t i", i=4),
+        in_=raw_pass[:, :, :VECTOR_COLS].rearrange("p t (c i) -> p c t i", i=4),
+    )
+    nc.scalar.copy(
+        out=grouped[:, VECTOR_COLS:, :].rearrange("p (c i) t -> p c t i", i=4),
+        in_=raw_pass[:, :, VECTOR_COLS:].rearrange("p t (c i) -> p c t i", i=4),
+    )
+    nc.vector.quantize_mx(
+        out=codes.bitcast(FP8X4),
+        scales=scales,
+        in_=grouped[:].rearrange("p c t -> p (c t)"),
+    )
+
+
+def transpose_and_quantise(nc, psum, stage, words, ident, codes, scales):
+    turned = psum.tile([P, PASSES, 2, P], F32, name="turned")
+    for g in range(PASSES):
+        for u in range(2):
+            first = (2 * g + u) * P
+            nc.tensor.transpose(turned[:, g, u, :], words[:, first : first + P], ident[:])
+    grouped = stage.tile([P, PASSES * P * PACK], BF16, name="a_grouped", align_bytes=64)
+    nc.scalar.copy(
+        out=grouped[:].bitcast(F32).rearrange("p (g r u) -> p g r u", g=PASSES, u=2),
+        in_=turned[:].rearrange("p g u r -> p g r u"),
+    )
+    nc.vector.quantize_mx(
+        out=codes.rearrange("p g r -> p (g r)").bitcast(FP8X4),
+        scales=scales.rearrange("p g r -> p (g r)"),
+        in_=grouped[:],
+    )
+
+
+def mx_product(nc, acc, a_codes, a_scales, w_codes, w_scales):
+    for g in range(PASSES):
+        nc.tensor.matmul_mx(
+            out=acc,
+            lhsT=a_codes[:, g, :].bitcast(FP8X4),
+            lhsT_scale=a_scales[:, g, :],
+            rhs=w_codes[:, g, :].bitcast(FP8X4),
+            rhs_scale=w_scales[:, g, :],
+            start=(g == 0),
+            stop=(g == PASSES - 1),
+        )
 
 
 def tile_childsumtreelstmcell_pa_kernel(tc, x, child_h, child_c, Wf, bWf, Uf, bUf, out):
@@ -38,17 +96,18 @@ def tile_childsumtreelstmcell_pa_kernel(tc, x, child_h, child_c, Wf, bWf, Uf, bU
     with ExitStack() as stack:
         const = stack.enter_context(tc.tile_pool(name="const", bufs=1))
         inputs = stack.enter_context(tc.tile_pool(name="inputs", bufs=1))
+        raws = stack.enter_context(tc.tile_pool(name="raws", bufs=2 * H_HALVES))
+        cells = stack.enter_context(tc.tile_pool(name="cells", bufs=H_HALVES * NODE_BLOCKS))
         keep = stack.enter_context(tc.tile_pool(name="keep", bufs=1))
-        stage = stack.enter_context(tc.tile_pool(name="stage", bufs=2))
-        work = stack.enter_context(tc.tile_pool(name="work", bufs=3))
+        stage = stack.enter_context(tc.tile_pool(name="stage", bufs=3))
+        work = stack.enter_context(tc.tile_pool(name="work", bufs=4))
         psum_turn = stack.enter_context(tc.psum_pool(name="psum_turn", bufs=2))
-        psum_acc = stack.enter_context(tc.psum_pool(name="psum_acc", bufs=4))
-        psum_one = stack.enter_context(tc.psum_pool(name="psum_one", bufs=1))
-        stack.enter_context(tc.manual_schedule())
+        psum_acc = stack.enter_context(tc.psum_pool(name="psum_acc", bufs=3))
+        psum_sum = stack.enter_context(tc.psum_pool(name="psum_sum", bufs=2))
+        psum_back = stack.enter_context(tc.psum_pool(name="psum_back", bufs=1))
 
         halves = [slice(N_TILE * hh, N_TILE * (hh + 1)) for hh in range(H_HALVES)]
         node_rows = [slice(P * nb, P * (nb + 1)) for nb in range(NODE_BLOCKS)]
-        weights = {"wf": Wf, "uf": Uf}
 
         ident = const.tile([P, P], F32, name="ident")
         make_identity(nc, ident[:])
@@ -61,22 +120,8 @@ def tile_childsumtreelstmcell_pa_kernel(tc, x, child_h, child_c, Wf, bWf, Uf, bU
 
         x_sb = inputs.tile([P, NODE_BLOCKS * D], BF16, name="x_sb")
         h_sb = [inputs.tile([P, CHILDREN * D], BF16, name="h_sb%d" % nb) for nb in range(NODE_BLOCKS)]
-        c_sb = {}
         w_raw = {}
-        for hh in range(H_HALVES):
-            for nb in range(NODE_BLOCKS):
-                c_sb[hh, nb] = inputs.tile([P, CHILDREN, N_TILE], BF16, name="c_sb%d%d" % (hh, nb))
-            for name in weights:
-                w_raw[name, hh] = inputs.tile([P, PASSES, PACK, N_TILE], BF16, name="%s_raw%d" % (name, hh))
-
-        def load_weight_half(name, hh):
-            for g in range(PASSES):
-                for u in range(2):
-                    first = K_PASS * g + PAIR_ROWS * u
-                    nc.sync.dma_start(
-                        out=w_raw[name, hh][:, g, 2 * u : 2 * u + 2, :],
-                        in_=weights[name][first : first + PAIR_ROWS, halves[hh]].rearrange("(q e) c -> q e c", e=2),
-                    )
+        c_sb = {}
 
         def load_children(nb, part):
             kids = slice(CHILDREN // 2 * part, CHILDREN // 2 * (part + 1))
@@ -87,6 +132,8 @@ def tile_childsumtreelstmcell_pa_kernel(tc, x, child_h, child_c, Wf, bWf, Uf, bU
 
         def load_cells(hh, nb, part):
             kids = slice(CHILDREN // 2 * part, CHILDREN // 2 * (part + 1))
+            if part == 0:
+                c_sb[hh, nb] = cells.tile([P, CHILDREN, N_TILE], BF16, name="c_sb")
             nc.sync.dma_start(out=c_sb[hh, nb][:, kids, :], in_=child_c[node_rows[nb], kids, halves[hh]])
 
         nc.sync.dma_start(
@@ -95,17 +142,17 @@ def tile_childsumtreelstmcell_pa_kernel(tc, x, child_h, child_c, Wf, bWf, Uf, bU
         )
         nc.sync.dma_start(out=bias_rows[0:1, :], in_=bWf.unsqueeze(0))
         nc.sync.dma_start(out=bias_rows[1:2, :], in_=bUf.unsqueeze(0))
-        load_weight_half("wf", 0)
-        load_weight_half("uf", 0)
+        w_raw["wf", 0] = load_weight_half(nc, raws, Wf, halves[0])
         load_children(0, 0)
+        w_raw["uf", 0] = load_weight_half(nc, raws, Uf, halves[0])
         load_children(0, 1)
         load_cells(0, 0, 0)
         load_children(1, 0)
         load_cells(0, 0, 1)
-        load_weight_half("wf", 1)
+        w_raw["wf", 1] = load_weight_half(nc, raws, Wf, halves[1])
         load_children(1, 1)
         load_cells(0, 1, 0)
-        load_weight_half("uf", 1)
+        w_raw["uf", 1] = load_weight_half(nc, raws, Uf, halves[1])
         load_cells(0, 1, 1)
         for nb in range(NODE_BLOCKS):
             for part in range(2):
@@ -113,202 +160,83 @@ def tile_childsumtreelstmcell_pa_kernel(tc, x, child_h, child_c, Wf, bWf, Uf, bU
 
         w_codes = {}
         w_scales = {}
-        for name in weights:
+        for name in ("wf", "uf"):
             w_codes[name] = keep.tile([P, H_HALVES, PASSES, N_TILE], U32, name=name + "_codes", align_bytes=64)
             w_scales[name] = keep.tile([P, H_HALVES, PASSES, N_TILE], U8, name=name + "_scales", align_bytes=64)
         x_codes = keep.tile([P, NODE_BLOCKS, PASSES, P], U32, name="x_codes", align_bytes=64)
         x_scales = keep.tile([P, NODE_BLOCKS, PASSES, P], U8, name="x_scales", align_bytes=64)
-        h_codes = keep.tile([P, NODE_BLOCKS * CHILDREN, PASSES, P], U32, name="h_codes", align_bytes=64)
-        h_scales = keep.tile([P, NODE_BLOCKS * CHILDREN, PASSES, P], U8, name="h_scales", align_bytes=64)
-        bias_sb = keep.tile([P, H], F32, name="bias_sb")
-        xfb = keep.tile([P, NODE_BLOCKS, H], F32, name="xfb")
+        h_codes = keep.tile([P, NODE_BLOCKS, CHILDREN, PASSES, P], U32, name="h_codes", align_bytes=64)
+        h_scales = keep.tile([P, NODE_BLOCKS, CHILDREN, PASSES, P], U8, name="h_scales", align_bytes=64)
 
-        turned = {}
-        a_grouped = {}
-        w_grouped = {}
-        acc = {}
-        z = {}
-        gate = {}
-        weighted = {}
-        summed_t = {}
-        summed_t_sb = {}
-        result_ps = {}
+        def prepare_weight_pass(name, hh, g):
+            quantise_weight_pass(nc, stage, w_raw[name, hh][:, g], w_codes[name][:, hh, g, :], w_scales[name][:, hh, g, :])
+
         words_per_row = D // 2
 
-        def turn(key, words):
-            for i in range(2):
-                turned[key, i] = psum_turn.tile([P, PASSES, 2, P], F32, name="turned")
-                for g in range(PASSES):
-                    for u in range(2):
-                        first = words_per_row * i + (2 * g + u) * P
-                        nc.tensor.transpose(turned[key, i][:, g, u, :], words[:, first : first + P], ident[:])
+        def prepare_child(nb, k):
+            words = h_sb[nb][:].bitcast(F32)[:, words_per_row * k : words_per_row * (k + 1)]
+            transpose_and_quantise(nc, psum_turn, stage, words, ident, h_codes[:, nb, k], h_scales[:, nb, k])
 
-        def regroup_turned(key):
-            a_grouped[key] = stage.tile([P, 2 * PASSES * P * PACK], BF16, name="a_grouped", align_bytes=64)
-            pairs_of_words = a_grouped[key][:].bitcast(F32).rearrange("p (i g r u) -> p i g r u", i=2, g=PASSES, u=2)
-            for i in range(2):
-                nc.scalar.copy(out=pairs_of_words[:, i], in_=turned[key, i][:].rearrange("p g u r -> p g r u"))
-
-        def quantise_turned(key, codes, scales):
-            nc.vector.quantize_mx(
-                out=codes.rearrange("p i g r -> p (i g r)").bitcast(FP8X4),
-                scales=scales.rearrange("p i g r -> p (i g r)"),
-                in_=a_grouped[key][:],
-            )
-
-        def weight_pass(piece):
-            return ("wf", "uf")[piece // PASSES % 2], piece // (2 * PASSES), piece % PASSES
-
-        def regroup_weights(piece):
-            name, hh, g = weight_pass(piece)
-            w_grouped[piece] = stage.tile([P, N_TILE, PACK], BF16, name="w_grouped", align_bytes=64)
-            nc.vector.tensor_copy(
-                out=w_grouped[piece][:, :VECTOR_COLS, :].rearrange("p (c i) t -> p c t i", i=4),
-                in_=w_raw[name, hh][:, g, :, :VECTOR_COLS].rearrange("p t (c i) -> p c t i", i=4),
-            )
-            nc.scalar.copy(
-                out=w_grouped[piece][:, VECTOR_COLS:, :].rearrange("p (c i) t -> p c t i", i=4),
-                in_=w_raw[name, hh][:, g, :, VECTOR_COLS:].rearrange("p t (c i) -> p c t i", i=4),
-            )
-
-        def quantise_weights(piece):
-            name, hh, g = weight_pass(piece)
-            nc.vector.quantize_mx(
-                out=w_codes[name][:, hh, g, :].bitcast(FP8X4),
-                scales=w_scales[name][:, hh, g, :],
-                in_=w_grouped[piece][:].rearrange("p c t -> p (c t)"),
-            )
-
-        def mx_product(bank, a_codes, a_scales, name, hh):
-            for g in range(PASSES):
-                nc.tensor.matmul_mx(
-                    out=bank,
-                    lhsT=a_codes[:, g, :].bitcast(FP8X4),
-                    lhsT_scale=a_scales[:, g, :],
-                    rhs=w_codes[name][:, hh, g, :].bitcast(FP8X4),
-                    rhs_scale=w_scales[name][:, hh, g, :],
-                    start=(g == 0),
-                    stop=(g == PASSES - 1),
-                )
-
-        def place(pair):
-            unit = pair // PAIRS_PER_UNIT
-            return unit, unit // NODE_BLOCKS, unit % NODE_BLOCKS, 2 * (pair % PAIRS_PER_UNIT)
-
-        def turn_children(pair):
-            if 0 <= pair < NODE_BLOCKS * PAIRS_PER_UNIT:
-                unit, hh, nb, first_child = place(pair)
-                turn(pair, h_sb[nb][:].bitcast(F32)[:, words_per_row * first_child : words_per_row * (first_child + 2)])
-
-        def regroup_children(pair):
-            if 0 <= pair < NODE_BLOCKS * PAIRS_PER_UNIT:
-                regroup_turned(pair)
-
-        def quantise_children(pair):
-            if 0 <= pair < NODE_BLOCKS * PAIRS_PER_UNIT:
-                quantise_turned(pair, h_codes[:, 2 * pair : 2 * pair + 2], h_scales[:, 2 * pair : 2 * pair + 2])
-
-        def multiply(pair):
-            if 0 <= pair < PAIRS:
-                unit, hh, nb, first_child = place(pair)
-                if first_child == 0:
-                    acc["x", unit] = psum_one.tile([P, N_TILE], F32, name="lone")
-                    mx_product(acc["x", unit][:], x_codes[:, nb], x_scales[:, nb], "wf", hh)
-                for i in range(2):
-                    child = CHILDREN * nb + first_child + i
-                    acc[pair, i] = psum_acc.tile([P, N_TILE], F32, name="acc")
-                    mx_product(acc[pair, i][:], h_codes[:, child], h_scales[:, child], "uf", hh)
-
-        def add_x(pair):
-            if 0 <= pair < PAIRS:
-                unit, hh, nb, first_child = place(pair)
-                if first_child == 0:
-                    nc.vector.tensor_tensor(
-                        out=xfb[:, nb, halves[hh]], in0=acc["x", unit][:], in1=bias_sb[:, halves[hh]], op=ADD
-                    )
-                z[pair] = work.tile([P, 2, N_TILE], F32, name="z")
-                for i in range(2):
-                    nc.vector.tensor_tensor(out=z[pair][:, i, :], in0=acc[pair, i][:], in1=xfb[:, nb, halves[hh]], op=ADD)
-
-        def squash(pair):
-            if 0 <= pair < PAIRS:
-                gate[pair] = work.tile([P, 2, N_TILE], F32, name="gate")
-                nc.scalar.activation(out=gate[pair][:], in_=z[pair][:], func=SIGMOID)
-
-        def weigh(pair):
-            if 0 <= pair < PAIRS:
-                unit, hh, nb, first_child = place(pair)
-                weighted[pair] = work.tile([P, 2, N_TILE], F32, name="weighted")
-                nc.vector.tensor_tensor(
-                    out=weighted[pair][:], in0=gate[pair][:], in1=c_sb[hh, nb][:, first_child : first_child + 2, :], op=MULT
-                )
-
-        def sum_children(pair):
-            if 0 <= pair < PAIRS:
-                unit, hh, nb, first_child = place(pair)
-                if first_child == 0:
-                    summed_t[unit] = psum_one.tile([P, BLOCKS, P], F32, name="summed_t")
-                for i in range(2):
-                    for j in range(BLOCKS):
-                        nc.tensor.matmul(
-                            out=summed_t[unit][:, j, :],
-                            lhsT=weighted[pair][:, i, P * j : P * (j + 1)],
-                            rhs=ident[:],
-                            is_transpose=True,
-                            start=(first_child + i == 0 and j == 0),
-                            stop=(first_child + i == CHILDREN - 1 and j == BLOCKS - 1),
-                        )
-
-        def is_last_of_unit(pair):
-            return 0 <= pair < PAIRS and pair % PAIRS_PER_UNIT == PAIRS_PER_UNIT - 1
-
-        def copy_sum(pair):
-            if is_last_of_unit(pair):
-                unit = pair // PAIRS_PER_UNIT
-                summed_t_sb[unit] = work.tile([P, BLOCKS, P], F32, name="summed_t_sb")
-                nc.scalar.copy(out=summed_t_sb[unit][:], in_=summed_t[unit][:])
-
-        def turn_sum_back(pair):
-            if is_last_of_unit(pair):
-                unit = pair // PAIRS_PER_UNIT
-                result_ps[unit] = psum_one.tile([P, N_TILE], F32, name="lone")
-                for j in range(BLOCKS):
-                    nc.tensor.transpose(result_ps[unit][:, P * j : P * (j + 1)], summed_t_sb[unit][:, j, :], ident[:])
-
-        def store(pair):
-            if is_last_of_unit(pair):
-                unit, hh, nb, first_child = place(pair)
-                result = work.tile([P, N_TILE], F32, name="result")
-                nc.scalar.copy(out=result[:], in_=result_ps[unit][:])
-                nc.sync.dma_start(out=out[node_rows[nb], halves[hh]], in_=result[:])
-
-        turn("x", x_sb[:].bitcast(F32))
-        regroup_turned("x")
-        quantise_turned("x", x_codes[:], x_scales[:])
+        bias_sb = keep.tile([P, H], F32, name="bias_sb")
         for hh in range(H_HALVES):
             bias_ps = psum_acc.tile([P, N_TILE], F32, name="acc")
             nc.tensor.matmul(out=bias_ps[:], lhsT=ones[:], rhs=bias_rows[:, halves[hh]], start=True, stop=True)
             nc.scalar.copy(out=bias_sb[:, halves[hh]], in_=bias_ps[:])
-        for piece in range(2 * PASSES + 1):
-            if piece < 2 * PASSES:
-                regroup_weights(piece)
-            if piece > 0:
-                quantise_weights(piece - 1)
 
-        for now in range(-4, PAIRS + 3):
-            sum_children(now - 1)
-            turn_sum_back(now - 2)
-            multiply(now + 2)
-            regroup_children(now + 3)
-            turn_children(now + 4)
-            add_x(now + 1)
-            late_piece = now + LATE_WEIGHTS
-            if 2 * PASSES <= late_piece < 4 * PASSES:
-                regroup_weights(late_piece)
-            squash(now + 1)
-            weigh(now)
-            quantise_children(now + 3)
-            if 2 * PASSES <= late_piece < 4 * PASSES:
-                quantise_weights(late_piece)
-            copy_sum(now - 1)
-            store(now - 2)
+        for nb in range(NODE_BLOCKS):
+            words = x_sb[:].bitcast(F32)[:, words_per_row * nb : words_per_row * (nb + 1)]
+            transpose_and_quantise(nc, psum_turn, stage, words, ident, x_codes[:, nb], x_scales[:, nb])
+        for name in ("wf", "uf"):
+            for g in range(PASSES):
+                prepare_weight_pass(name, 0, g)
+        for k in range(AHEAD):
+            prepare_child(0, k)
+
+        xfb = keep.tile([P, NODE_BLOCKS, H], F32, name="xfb")
+        summed_t = None
+
+        for step in range(H_HALVES * NODE_BLOCKS * CHILDREN):
+            hh = step // (NODE_BLOCKS * CHILDREN)
+            nb = step // CHILDREN % NODE_BLOCKS
+            k = step % CHILDREN
+
+            if k == 0:
+                xf_ps = psum_acc.tile([P, N_TILE], F32, name="acc")
+                mx_product(nc, xf_ps[:], x_codes[:, nb], x_scales[:, nb], w_codes["wf"][:, hh], w_scales["wf"][:, hh])
+                nc.vector.tensor_tensor(out=xfb[:, nb, halves[hh]], in0=xf_ps[:], in1=bias_sb[:, halves[hh]], op=ADD)
+                summed_t = psum_sum.tile([P, BLOCKS, P], F32, name="summed_t")
+
+            hf_ps = psum_acc.tile([P, N_TILE], F32, name="acc")
+            mx_product(nc, hf_ps[:], h_codes[:, nb, k], h_scales[:, nb, k], w_codes["uf"][:, hh], w_scales["uf"][:, hh])
+            z = work.tile([P, N_TILE], F32, name="z")
+            nc.vector.tensor_tensor(out=z[:], in0=hf_ps[:], in1=xfb[:, nb, halves[hh]], op=ADD)
+            gate = work.tile([P, N_TILE], F32, name="gate")
+            nc.scalar.activation(out=gate[:], in_=z[:], func=SIGMOID)
+            weighted = work.tile([P, N_TILE], F32, name="weighted")
+            nc.vector.tensor_tensor(out=weighted[:], in0=gate[:], in1=c_sb[hh, nb][:, k, :], op=MULT)
+
+            for j in range(BLOCKS):
+                nc.tensor.matmul(
+                    out=summed_t[:, j, :],
+                    lhsT=weighted[:, P * j : P * (j + 1)],
+                    rhs=ident[:],
+                    is_transpose=True,
+                    start=(k == 0 and j == 0),
+                    stop=(k == CHILDREN - 1 and j == BLOCKS - 1),
+                )
+
+            if k == CHILDREN - 1:
+                summed_t_sb = work.tile([P, BLOCKS, P], F32, name="summed_t_sb")
+                nc.scalar.copy(out=summed_t_sb[:], in_=summed_t[:])
+                result_ps = psum_back.tile([P, N_TILE], F32, name="result_ps")
+                for j in range(BLOCKS):
+                    nc.tensor.transpose(result_ps[:, P * j : P * (j + 1)], summed_t_sb[:, j, :], ident[:])
+                result = work.tile([P, N_TILE], F32, name="result")
+                nc.scalar.copy(out=result[:], in_=result_ps[:])
+                nc.sync.dma_start(out=out[node_rows[nb], halves[hh]], in_=result[:])
+
+            child = step + AHEAD
+            if child < NODE_BLOCKS * CHILDREN:
+                prepare_child(child // CHILDREN, child % CHILDREN)
+            if hh == 0 and step % 4 == 3:
+                prepare_weight_pass(("wf", "uf")[step // 8], 1, step // 4 % PASSES)

from contextlib import ExitStack

import concourse.mybir as mybir
from concourse.masks import make_identity

F32 = mybir.dt.float32
BF16 = mybir.dt.bfloat16
U32 = mybir.dt.uint32
U8 = mybir.dt.uint8
FP8X4 = mybir.dt.float8_e4m3fn_x4
ADD = mybir.AluOpType.add
MULT = mybir.AluOpType.mult
SIGMOID = mybir.ActivationFunctionType.Sigmoid

P = 128
NODES = 256
CHILDREN = 8
D = 1024
H = 1024
PACK = 4
K_PASS = P * PACK
PASSES = D // K_PASS
PAIR_ROWS = 2 * P
N_TILE = 512
H_HALVES = H // N_TILE
NODE_BLOCKS = NODES // P
BLOCKS = N_TILE // P

FLOPS = 2 * (NODES + NODES * CHILDREN) * D * H
VECTOR_COLS = 256
AHEAD = 6


def load_weight_half(nc, pool, w, cols):
    raw = pool.tile([P, PASSES, PACK, N_TILE], BF16, name="w_raw")
    for g in range(PASSES):
        for u in range(2):
            first = K_PASS * g + PAIR_ROWS * u
            nc.sync.dma_start(
                out=raw[:, g, 2 * u : 2 * u + 2, :],
                in_=w[first : first + PAIR_ROWS, cols].rearrange("(q e) c -> q e c", e=2),
            )
    return raw


def quantise_weight_pass(nc, stage, raw_pass, codes, scales):
    grouped = stage.tile([P, N_TILE, PACK], BF16, name="w_grouped", align_bytes=64)
    nc.vector.tensor_copy(
        out=grouped[:, :VECTOR_COLS, :].rearrange("p (c i) t -> p c t i", i=4),
        in_=raw_pass[:, :, :VECTOR_COLS].rearrange("p t (c i) -> p c t i", i=4),
    )
    nc.scalar.copy(
        out=grouped[:, VECTOR_COLS:, :].rearrange("p (c i) t -> p c t i", i=4),
        in_=raw_pass[:, :, VECTOR_COLS:].rearrange("p t (c i) -> p c t i", i=4),
    )
    nc.vector.quantize_mx(
        out=codes.bitcast(FP8X4),
        scales=scales,
        in_=grouped[:].rearrange("p c t -> p (c t)"),
    )


def transpose_and_quantise(nc, psum, stage, words, ident, codes, scales):
    turned = psum.tile([P, PASSES, 2, P], F32, name="turned")
    for g in range(PASSES):
        for u in range(2):
            first = (2 * g + u) * P
            nc.tensor.transpose(turned[:, g, u, :], words[:, first : first + P], ident[:])
    grouped = stage.tile([P, PASSES * P * PACK], BF16, name="a_grouped", align_bytes=64)
    nc.scalar.copy(
        out=grouped[:].bitcast(F32).rearrange("p (g r u) -> p g r u", g=PASSES, u=2),
        in_=turned[:].rearrange("p g u r -> p g r u"),
    )
    nc.vector.quantize_mx(
        out=codes.rearrange("p g r -> p (g r)").bitcast(FP8X4),
        scales=scales.rearrange("p g r -> p (g r)"),
        in_=grouped[:],
    )


def mx_product(nc, acc, a_codes, a_scales, w_codes, w_scales):
    for g in range(PASSES):
        nc.tensor.matmul_mx(
            out=acc,
            lhsT=a_codes[:, g, :].bitcast(FP8X4),
            lhsT_scale=a_scales[:, g, :],
            rhs=w_codes[:, g, :].bitcast(FP8X4),
            rhs_scale=w_scales[:, g, :],
            start=(g == 0),
            stop=(g == PASSES - 1),
        )


def tile_childsumtreelstmcell_pa_kernel(tc, x, child_h, child_c, Wf, bWf, Uf, bUf, out):
    nc = tc.nc
    with ExitStack() as stack:
        const = stack.enter_context(tc.tile_pool(name="const", bufs=1))
        inputs = stack.enter_context(tc.tile_pool(name="inputs", bufs=1))
        raws = stack.enter_context(tc.tile_pool(name="raws", bufs=2 * H_HALVES))
        cells = stack.enter_context(tc.tile_pool(name="cells", bufs=H_HALVES * NODE_BLOCKS))
        keep = stack.enter_context(tc.tile_pool(name="keep", bufs=1))
        stage = stack.enter_context(tc.tile_pool(name="stage", bufs=3))
        work = stack.enter_context(tc.tile_pool(name="work", bufs=4))
        psum_turn = stack.enter_context(tc.psum_pool(name="psum_turn", bufs=2))
        psum_acc = stack.enter_context(tc.psum_pool(name="psum_acc", bufs=3))
        psum_sum = stack.enter_context(tc.psum_pool(name="psum_sum", bufs=2))
        psum_back = stack.enter_context(tc.psum_pool(name="psum_back", bufs=1))

        halves = [slice(N_TILE * hh, N_TILE * (hh + 1)) for hh in range(H_HALVES)]
        node_rows = [slice(P * nb, P * (nb + 1)) for nb in range(NODE_BLOCKS)]

        ident = const.tile([P, P], F32, name="ident")
        make_identity(nc, ident[:])
        ones = const.tile([P, P], BF16, name="ones")
        nc.vector.memset(ones[:], 1.0)
        bias_rows = const.tile([P, H], BF16, name="bias_rows")
        nc.vector.memset(bias_rows[:], 0.0)
        warm = const.tile([P, 1], F32, name="warm")
        nc.scalar.activation(out=warm[:], in_=ones[:, 0:1], func=SIGMOID)

        x_sb = inputs.tile([P, NODE_BLOCKS * D], BF16, name="x_sb")
        h_sb = [inputs.tile([P, CHILDREN * D], BF16, name="h_sb%d" % nb) for nb in range(NODE_BLOCKS)]
        w_raw = {}
        c_sb = {}

        def load_children(nb, part):
            kids = slice(CHILDREN // 2 * part, CHILDREN // 2 * (part + 1))
            nc.sync.dma_start(
                out=h_sb[nb][:].rearrange("p (k d) -> p k d", k=CHILDREN)[:, kids, :],
                in_=child_h[node_rows[nb], kids, :],
            )

        def load_cells(hh, nb, part):
            kids = slice(CHILDREN // 2 * part, CHILDREN // 2 * (part + 1))
            if part == 0:
                c_sb[hh, nb] = cells.tile([P, CHILDREN, N_TILE], BF16, name="c_sb")
            nc.sync.dma_start(out=c_sb[hh, nb][:, kids, :], in_=child_c[node_rows[nb], kids, halves[hh]])

        nc.sync.dma_start(
            out=x_sb[:].rearrange("p (b d) -> p b d", b=NODE_BLOCKS),
            in_=x.rearrange("(b p) d -> p b d", p=P),
        )
        nc.sync.dma_start(out=bias_rows[0:1, :], in_=bWf.unsqueeze(0))
        nc.sync.dma_start(out=bias_rows[1:2, :], in_=bUf.unsqueeze(0))
        w_raw["wf", 0] = load_weight_half(nc, raws, Wf, halves[0])
        load_children(0, 0)
        w_raw["uf", 0] = load_weight_half(nc, raws, Uf, halves[0])
        load_children(0, 1)
        load_cells(0, 0, 0)
        load_children(1, 0)
        load_cells(0, 0, 1)
        w_raw["wf", 1] = load_weight_half(nc, raws, Wf, halves[1])
        load_children(1, 1)
        load_cells(0, 1, 0)
        w_raw["uf", 1] = load_weight_half(nc, raws, Uf, halves[1])
        load_cells(0, 1, 1)
        for nb in range(NODE_BLOCKS):
            for part in range(2):
                load_cells(1, nb, part)

        w_codes = {}
        w_scales = {}
        for name in ("wf", "uf"):
            w_codes[name] = keep.tile([P, H_HALVES, PASSES, N_TILE], U32, name=name + "_codes", align_bytes=64)
            w_scales[name] = keep.tile([P, H_HALVES, PASSES, N_TILE], U8, name=name + "_scales", align_bytes=64)
        x_codes = keep.tile([P, NODE_BLOCKS, PASSES, P], U32, name="x_codes", align_bytes=64)
        x_scales = keep.tile([P, NODE_BLOCKS, PASSES, P], U8, name="x_scales", align_bytes=64)
        h_codes = keep.tile([P, NODE_BLOCKS, CHILDREN, PASSES, P], U32, name="h_codes", align_bytes=64)
        h_scales = keep.tile([P, NODE_BLOCKS, CHILDREN, PASSES, P], U8, name="h_scales", align_bytes=64)

        def prepare_weight_pass(name, hh, g):
            quantise_weight_pass(nc, stage, w_raw[name, hh][:, g], w_codes[name][:, hh, g, :], w_scales[name][:, hh, g, :])

        words_per_row = D // 2

        def prepare_child(nb, k):
            words = h_sb[nb][:].bitcast(F32)[:, words_per_row * k : words_per_row * (k + 1)]
            transpose_and_quantise(nc, psum_turn, stage, words, ident, h_codes[:, nb, k], h_scales[:, nb, k])

        bias_sb = keep.tile([P, H], F32, name="bias_sb")
        for hh in range(H_HALVES):
            bias_ps = psum_acc.tile([P, N_TILE], F32, name="acc")
            nc.tensor.matmul(out=bias_ps[:], lhsT=ones[:], rhs=bias_rows[:, halves[hh]], start=True, stop=True)
            nc.scalar.copy(out=bias_sb[:, halves[hh]], in_=bias_ps[:])

        for nb in range(NODE_BLOCKS):
            words = x_sb[:].bitcast(F32)[:, words_per_row * nb : words_per_row * (nb + 1)]
            transpose_and_quantise(nc, psum_turn, stage, words, ident, x_codes[:, nb], x_scales[:, nb])
        for name in ("wf", "uf"):
            for g in range(PASSES):
                prepare_weight_pass(name, 0, g)
        for k in range(AHEAD):
            prepare_child(0, k)

        xfb = keep.tile([P, NODE_BLOCKS, H], F32, name="xfb")
        summed_t = None

        for step in range(H_HALVES * NODE_BLOCKS * CHILDREN):
            hh = step // (NODE_BLOCKS * CHILDREN)
            nb = step // CHILDREN % NODE_BLOCKS
            k = step % CHILDREN

            if k == 0:
                xf_ps = psum_acc.tile([P, N_TILE], F32, name="acc")
                mx_product(nc, xf_ps[:], x_codes[:, nb], x_scales[:, nb], w_codes["wf"][:, hh], w_scales["wf"][:, hh])
                nc.vector.tensor_tensor(out=xfb[:, nb, halves[hh]], in0=xf_ps[:], in1=bias_sb[:, halves[hh]], op=ADD)
                summed_t = psum_sum.tile([P, BLOCKS, P], F32, name="summed_t")

            hf_ps = psum_acc.tile([P, N_TILE], F32, name="acc")
            mx_product(nc, hf_ps[:], h_codes[:, nb, k], h_scales[:, nb, k], w_codes["uf"][:, hh], w_scales["uf"][:, hh])
            z = work.tile([P, N_TILE], F32, name="z")
            nc.vector.tensor_tensor(out=z[:], in0=hf_ps[:], in1=xfb[:, nb, halves[hh]], op=ADD)
            gate = work.tile([P, N_TILE], F32, name="gate")
            nc.scalar.activation(out=gate[:], in_=z[:], func=SIGMOID)
            weighted = work.tile([P, N_TILE], F32, name="weighted")
            nc.vector.tensor_tensor(out=weighted[:], in0=gate[:], in1=c_sb[hh, nb][:, k, :], op=MULT)

            for j in range(BLOCKS):
                nc.tensor.matmul(
                    out=summed_t[:, j, :],
                    lhsT=weighted[:, P * j : P * (j + 1)],
                    rhs=ident[:],
                    is_transpose=True,
                    start=(k == 0 and j == 0),
                    stop=(k == CHILDREN - 1 and j == BLOCKS - 1),
                )

            if k == CHILDREN - 1:
                summed_t_sb = work.tile([P, BLOCKS, P], F32, name="summed_t_sb")
                nc.scalar.copy(out=summed_t_sb[:], in_=summed_t[:])
                result_ps = psum_back.tile([P, N_TILE], F32, name="result_ps")
                for j in range(BLOCKS):
                    nc.tensor.transpose(result_ps[:, P * j : P * (j + 1)], summed_t_sb[:, j, :], ident[:])
                result = work.tile([P, N_TILE], F32, name="result")
                nc.scalar.copy(out=result[:], in_=result_ps[:])
                nc.sync.dma_start(out=out[node_rows[nb], halves[hh]], in_=result[:])

            child = step + AHEAD
            if child < NODE_BLOCKS * CHILDREN:
                prepare_child(child // CHILDREN, child % CHILDREN)
            if hh == 0 and step % 4 == 3:
                prepare_weight_pass(("wf", "uf")[step // 8], 1, step // 4 % PASSES)
